import numpy as np
import ml_dtypes


def mxq(x, axis, fmt="e4m3"):
    dtype, down = {"e4m3": (ml_dtypes.float8_e4m3fn, 7), "e5m2": (ml_dtypes.float8_e5m2, 14)}[fmt]
    v = np.moveaxis(np.asarray(x, np.float32).astype(ml_dtypes.bfloat16).astype(np.float64), axis, -1)
    blocks = v.reshape(v.shape[:-1] + (-1, 32))
    amax = np.abs(blocks).max(-1, keepdims=True)
    byte = np.maximum(np.where(amax > 0, np.frexp(amax)[1] - 1 + 127, 0) - down, 1)
    scale = np.exp2(byte - 127.0)
    codes = (blocks / scale).astype(np.float32).astype(dtype).astype(np.float64)
    return np.moveaxis((codes * scale).reshape(v.shape), -1, axis)


WIDE = False


def mx_kscale(k):
    if not WIDE:
        return np.ones(k)
    levels = np.array([10, -10, 5, -5, 0])
    a = np.random.permutation(np.resize(levels, k // 512 * 4)).reshape(k // 512, 4)
    idx = np.arange(k)
    return np.exp2(a[idx // 512, idx % 128 // 32])


BF16 = ml_dtypes.bfloat16


def bf(x):
    return np.asarray(x, np.float32).astype(BF16)


def f64(x):
    return np.asarray(x).astype(np.float64)


B, IN, H, OUT, L, STEPS = 4096, 512, 512, 128, 3, 3
LN_EPS = 1e-5
TAU_EPS = 1e-6


def layer_norm(v, g, b):
    m = v.mean(-1, keepdims=True)
    var = ((v - m) ** 2).mean(-1, keepdims=True)
    return (v - m) / np.sqrt(var + LN_EPS) * g + b


def setup_inputs():
    r = mx_kscale(IN)
    s = mx_kscale(H)
    s = s / s.max()
    t = mx_kscale(H)
    liq_rms = np.sqrt(L * (L + 1) / 2.0)
    return {"liq": bf(np.random.standard_normal((B, H)) * liq_rms * s),
            "h": bf(np.random.standard_normal((B, H))),
            "x": bf(np.random.standard_normal((B, IN)) * r),
            "W_in": bf(np.random.standard_normal((H, IN)) * 0.7 / np.sqrt(IN) / r),
            "b_in": bf(np.random.standard_normal(H) * 0.3),
            "W_v": bf(np.random.standard_normal((H, H)) / np.sqrt(H) * t[:, None] / s),
            "b_v": bf(np.random.standard_normal(H) * 0.5 * t),
            "W_o": bf(np.random.standard_normal((H, H)) / np.sqrt(H) / t),
            "b_o": bf(np.random.standard_normal(H) * 0.5),
            "g_att": bf(1.0 + 0.1 * np.random.standard_normal(H)),
            "beta_att": bf(np.random.standard_normal(H) * 0.3),
            "tau": bf(0.5 + 0.5 * np.random.random(H))}


def reference(liq, h, x, W_in, b_in, W_v, b_v, W_o, b_o, g_att, beta_att, tau):
    liq, h = f64(liq), f64(h)
    xin = (mxq(f64(x), 1, "e4m3") @ mxq(f64(W_in), 1, "e4m3").T) + f64(b_in)
    v = (mxq(liq, 1, "e4m3") @ mxq(f64(W_v), 1, "e4m3").T) + f64(b_v)
    att = (mxq(v, 1, "e4m3") @ mxq(f64(W_o), 1, "e4m3").T) + f64(b_o)
    z = layer_norm(att + liq, f64(g_att), f64(beta_att))
    dh = (-h + np.tanh(z + xin)) / (f64(tau) + TAU_EPS)
    return h + dh

@@ -1,0 +1,322 @@
+from contextlib import ExitStack
+
+import concourse.mybir as mybir
+from concourse.masks import make_identity
+
+F32 = mybir.dt.float32
+BF16 = mybir.dt.bfloat16
+U32 = mybir.dt.uint32
+U8 = mybir.dt.uint8
+FP8X4 = mybir.dt.float8_e4m3fn_x4
+ALU = mybir.AluOpType
+ACT = mybir.ActivationFunctionType
+
+P = 128
+B = 4096
+H = 512
+TILES = 4
+GROUP = TILES * P
+GROUPS = B // GROUP
+LN_EPS = 1e-5
+TAU_EPS = 1e-6
+
+FLOPS = 3 * 2 * B * H * H
+
+
+def tile_advancedliquidneuralnetwork_pb_t_kernel(
+    tc, liq, h, x, W_in, b_in, W_v, b_v, W_o, b_o, g_att, beta_att, tau, out
+):
+    nc = tc.nc
+
+    def group_rows(dram, g):
+        return dram[g * GROUP : (g + 1) * GROUP, :].rearrange("(p t) f -> p t f", t=TILES)
+
+    def contiguous_words(words, u):
+        return words[:, u * P : (u + 1) * P]
+
+    def alternate_words(words, u):
+        return words.rearrange("r (p u) -> r u p", u=2)[:, u, :]
+
+    with ExitStack() as whole:
+        consts = whole.enter_context(tc.tile_pool(name="consts", bufs=1))
+        kept = whole.enter_context(tc.tile_pool(name="kept", bufs=1))
+        rows = whole.enter_context(tc.tile_pool(name="rows", bufs=3))
+        stage = whole.enter_context(tc.tile_pool(name="stage", bufs=2))
+        codes = whole.enter_context(tc.tile_pool(name="codes", bufs=2))
+
+        ident_f32 = consts.tile([P, P], F32)
+        make_identity(nc, ident_f32[:])
+        ident_bf16 = consts.tile([P, P], BF16)
+        make_identity(nc, ident_bf16[:])
+
+        def quantise_k_last(src, pick_words, words_out, scales_out, turn_ps):
+            grouped = stage.tile([P, GROUP, 2], F32, align_bytes=64)
+            for pair in range(2):
+                turned = turn_ps.tile([P, 2, 2, P], F32)
+                for i in range(2):
+                    words = src[:, 2 * pair + i, :].bitcast(F32)
+                    for u in range(2):
+                        nc.tensor.transpose(
+                            out=turned[:, i, u, :], in_=pick_words(words, u), identity=ident_f32[:]
+                        )
+                nc.scalar.copy(
+                    out=grouped[:, 2 * pair * P : 2 * (pair + 1) * P, :].rearrange(
+                        "p (i c) u -> p i c u", i=2
+                    ),
+                    in_=turned[:].rearrange("p i u c -> p i c u"),
+                )
+            nc.vector.quantize_mx(
+                out=words_out[:].bitcast(FP8X4),
+                scales=scales_out[:],
+                in_=grouped[:].rearrange("p c u -> p (c u)").bitcast(BF16),
+            )
+
+        def quantise_weight(w_rows, pick_words, words_out, scales_out, turn_ps):
+            w_sb = stage.tile([P, TILES, H], BF16)
+            nc.sync.dma_start(out=w_sb[:], in_=w_rows)
+            quantise_k_last(w_sb, pick_words, words_out, scales_out, turn_ps)
+
+        def mx_pass(acc, stationary, stationary_scales, moving, moving_scales):
+            nc.tensor.matmul_mx(
+                out=acc,
+                lhsT=stationary.bitcast(FP8X4),
+                lhsT_scale=stationary_scales,
+                rhs=moving.bitcast(FP8X4),
+                rhs_scale=moving_scales,
+                start=True,
+                stop=True,
+            )
+
+        wv_words = consts.tile([P, H], U32, align_bytes=64)
+        wv_scales = consts.tile([P, H], U8, align_bytes=64)
+        wo_words = consts.tile([P, H], U32, align_bytes=64)
+        wo_scales = consts.tile([P, H], U8, align_bytes=64)
+        win_words = consts.tile([P, H], U32, align_bytes=64)
+        win_scales = consts.tile([P, H], U8, align_bytes=64)
+
+        u_groups = []
+        neg_means = []
+        sum_sq = kept.tile([P, GROUPS * TILES], F32)
+
+        with ExitStack() as first:
+            work = first.enter_context(tc.tile_pool(name="work_a", bufs=2))
+            turn_ps = first.enter_context(tc.psum_pool(name="turn_a", bufs=2))
+            vT_ps = first.enter_context(tc.psum_pool(name="vT", bufs=3))
+            att_ps = first.enter_context(tc.psum_pool(name="att", bufs=3))
+
+            quantise_weight(
+                W_v.rearrange("(p j) k -> p j k", j=TILES), contiguous_words, wv_words, wv_scales, turn_ps
+            )
+            bv_bf16 = consts.tile([P, TILES], BF16)
+            nc.sync.dma_start(out=bv_bf16[:], in_=b_v.rearrange("(p j) -> p j", j=TILES))
+            bv = consts.tile([P, TILES], F32)
+            nc.vector.tensor_copy(out=bv[:], in_=bv_bf16[:])
+            bo_all = consts.tile([P, H], BF16)
+            nc.sync.dma_start(out=bo_all[:], in_=b_o.partition_broadcast(P))
+            quantise_weight(
+                W_o.rearrange("(a p) k -> p a k", p=P), alternate_words, wo_words, wo_scales, turn_ps
+            )
+
+            for g in range(GROUPS):
+                liq_sb = rows.tile([P, TILES, H], BF16)
+                nc.sync.dma_start(out=liq_sb[:], in_=group_rows(liq, g))
+                liq_words = codes.tile([P, GROUP], U32, align_bytes=64)
+                liq_scales = codes.tile([P, GROUP], U8, align_bytes=64)
+                quantise_k_last(liq_sb, contiguous_words, liq_words, liq_scales, turn_ps)
+
+                liq_bo = work.tile([P, TILES, H], F32)
+                nc.vector.tensor_tensor(
+                    out=liq_bo[:],
+                    in0=liq_sb[:],
+                    in1=bo_all[:].unsqueeze(1).to_broadcast([P, TILES, H]),
+                    op=ALU.add,
+                )
+
+                vT = work.tile([P, TILES, GROUP], BF16)
+                for j in range(TILES):
+                    vT_acc = vT_ps.tile([P, GROUP], F32)
+                    mx_pass(
+                        vT_acc[:],
+                        wv_words[:, j * P : (j + 1) * P],
+                        wv_scales[:, j * P : (j + 1) * P],
+                        liq_words[:],
+                        liq_scales[:],
+                    )
+                    nc.scalar.activation(
+                        out=vT[:, j, :], in_=vT_acc[:], func=ACT.Identity, bias=bv[:, j : j + 1]
+                    )
+                v_grouped = work.tile([P, GROUP, TILES], BF16, align_bytes=64)
+                nc.vector.tensor_copy(out=v_grouped[:], in_=vT[:].rearrange("p j c -> p c j"))
+                v_words = codes.tile([P, GROUP], U32, align_bytes=64)
+                v_scales = codes.tile([P, GROUP], U8, align_bytes=64)
+                nc.vector.quantize_mx(
+                    out=v_words[:].bitcast(FP8X4),
+                    scales=v_scales[:],
+                    in_=v_grouped[:].rearrange("p c j -> p (c j)"),
+                )
+
+                u = kept.tile([P, TILES, H], F32, name="u%d" % g)
+                u_groups.append(u)
+                sum_u = work.tile([P, TILES], F32)
+                for t in range(TILES):
+                    att = att_ps.tile([P, H], F32)
+                    mx_pass(
+                        att[:],
+                        v_words[:, t * P : (t + 1) * P],
+                        v_scales[:, t * P : (t + 1) * P],
+                        wo_words[:],
+                        wo_scales[:],
+                    )
+                    nc.vector.scalar_tensor_tensor(
+                        out=u[:, t, :],
+                        in0=att[:],
+                        scalar=1.0,
+                        in1=liq_bo[:, t, :],
+                        op0=ALU.mult,
+                        op1=ALU.add,
+                        accum_out=sum_u[:, t : t + 1],
+                    )
+                neg_mean = kept.tile([P, TILES], F32, name="neg_mean%d" % g)
+                neg_means.append(neg_mean)
+                nc.vector.tensor_scalar_mul(out=neg_mean[:], in0=sum_u[:], scalar1=-1.0 / H)
+                for t in range(TILES):
+                    squares = work.tile([P, H], BF16)
+                    nc.scalar.activation(
+                        out=squares[:],
+                        in_=u[:, t, :],
+                        func=ACT.Square,
+                        bias=neg_mean[:, t : t + 1],
+                        accum_out=sum_sq[:, g * TILES + t : g * TILES + t + 1],
+                    )
+
+            quantise_weight(
+                W_in.rearrange("(a p) k -> p a k", p=P), contiguous_words, win_words, win_scales, turn_ps
+            )
+            g_all = consts.tile([P, H], BF16)
+            nc.sync.dma_start(out=g_all[:], in_=g_att.partition_broadcast(P))
+            vec_rows = consts.tile([P, P], BF16)
+            nc.vector.memset(vec_rows[:], 0.0)
+            for n, vec in enumerate((b_in, beta_att, tau)):
+                nc.sync.dma_start(
+                    out=vec_rows[n * TILES : (n + 1) * TILES, :], in_=vec.rearrange("(j p) -> j p", p=P)
+                )
+            vec_ps = turn_ps.tile([P, P], BF16, tag="turned")
+            nc.tensor.transpose(out=vec_ps[:], in_=vec_rows[:], identity=ident_bf16[:])
+            vec_cols = consts.tile([P, 3 * TILES], F32)
+            nc.vector.tensor_copy(out=vec_cols[:], in_=vec_ps[:, 0 : 3 * TILES])
+            tanh_bias = consts.tile([P, TILES], F32)
+            nc.vector.tensor_add(
+                out=tanh_bias[:], in0=vec_cols[:, 0:TILES], in1=vec_cols[:, TILES : 2 * TILES]
+            )
+            gate = consts.tile([P, TILES], F32)
+            nc.vector.tensor_scalar_add(
+                out=gate[:], in0=vec_cols[:, 2 * TILES : 3 * TILES], scalar1=TAU_EPS
+            )
+            nc.vector.reciprocal(out=gate[:], in_=gate[:])
+            keep = consts.tile([P, TILES], F32)
+            nc.vector.tensor_scalar(
+                out=keep[:], in0=gate[:], scalar1=-1.0, scalar2=1.0, op0=ALU.mult, op1=ALU.add
+            )
+
+        rstd = kept.tile([P, GROUPS * TILES], F32)
+        nc.vector.tensor_scalar(
+            out=rstd[:], in0=sum_sq[:], scalar1=1.0 / H, scalar2=LN_EPS, op0=ALU.mult, op1=ALU.add
+        )
+        nc.scalar.sqrt(out=rstd[:], in_=rstd[:])
+        nc.vector.reciprocal(out=rstd[:], in_=rstd[:])
+
+        with ExitStack() as second:
+            work = second.enter_context(tc.tile_pool(name="work_c", bufs=2))
+            turn_ps = second.enter_context(tc.psum_pool(name="turn_c", bufs=1))
+            xin_ps = second.enter_context(tc.psum_pool(name="xin", bufs=2))
+            hT_ps = second.enter_context(tc.psum_pool(name="hT", bufs=2))
+            sT_ps = second.enter_context(tc.psum_pool(name="sT", bufs=2))
+            back_ps = second.enter_context(tc.psum_pool(name="back", bufs=1))
+
+            for g in range(GROUPS):
+                x_sb = rows.tile([P, TILES, H], BF16)
+                nc.sync.dma_start(out=x_sb[:], in_=group_rows(x, g))
+                h_sb = rows.tile([P, TILES, H], BF16)
+                nc.sync.dma_start(out=h_sb[:], in_=group_rows(h, g))
+                x_words = codes.tile([P, GROUP], U32, align_bytes=64)
+                x_scales = codes.tile([P, GROUP], U8, align_bytes=64)
+                quantise_k_last(x_sb, contiguous_words, x_words, x_scales, turn_ps)
+
+                hT = []
+                for pair in range(2):
+                    hT_pair = hT_ps.tile([P, 2, GROUP], BF16)
+                    hT.append(hT_pair)
+                    for i in range(2):
+                        j = 2 * pair + i
+                        for t in range(TILES):
+                            nc.tensor.transpose(
+                                out=hT_pair[:, i, t * P : (t + 1) * P],
+                                in_=h_sb[:, t, j * P : (j + 1) * P],
+                                identity=ident_bf16[:],
+                            )
+
+                u = u_groups[g]
+                s = work.tile([P, TILES, H], F32)
+                for t in range(TILES):
+                    xin = xin_ps.tile([P, H], F32)
+                    mx_pass(
+                        xin[:],
+                        x_words[:, t * P : (t + 1) * P],
+                        x_scales[:, t * P : (t + 1) * P],
+                        win_words[:],
+                        win_scales[:],
+                    )
+                    nc.vector.scalar_tensor_tensor(
+                        out=u[:, t, :],
+                        in0=u[:, t, :],
+                        scalar=neg_means[g][:, t : t + 1],
+                        in1=g_all[:],
+                        op0=ALU.add,
+                        op1=ALU.mult,
+                    )
+                    nc.vector.scalar_tensor_tensor(
+                        out=s[:, t, :],
+                        in0=u[:, t, :],
+                        scalar=rstd[:, g * TILES + t : g * TILES + t + 1],
+                        in1=xin[:],
+                        op0=ALU.mult,
+                        op1=ALU.add,
+                    )
+
+                tanhT = work.tile([P, TILES, GROUP], F32)
+                gatedT = work.tile([P, TILES, GROUP], F32)
+                outT = work.tile([P, TILES, GROUP], F32)
+                for j in range(TILES):
+                    sT = sT_ps.tile([P, GROUP], F32)
+                    for t in range(TILES):
+                        nc.tensor.transpose(
+                            out=sT[:, t * P : (t + 1) * P],
+                            in_=s[:, t, j * P : (j + 1) * P],
+                            identity=ident_f32[:],
+                        )
+                    nc.scalar.activation(
+                        out=tanhT[:, j, :], in_=sT[:], func=ACT.Tanh, bias=tanh_bias[:, j : j + 1]
+                    )
+                    nc.vector.tensor_scalar_mul(
+                        out=gatedT[:, j, :], in0=tanhT[:, j, :], scalar1=gate[:, j : j + 1]
+                    )
+                    nc.vector.scalar_tensor_tensor(
+                        out=outT[:, j, :],
+                        in0=hT[j // 2][:, j % 2, :],
+                        scalar=keep[:, j : j + 1],
+                        in1=gatedT[:, j, :],
+                        op0=ALU.mult,
+                        op1=ALU.add,
+                    )
+
+                out_sb = work.tile([P, TILES, H], F32)
+                for t in range(TILES):
+                    back = back_ps.tile([P, H], F32)
+                    for j in range(TILES):
+                        nc.tensor.transpose(
+                            out=back[:, j * P : (j + 1) * P],
+                            in_=outT[:, j, t * P : (t + 1) * P],
+                            identity=ident_f32[:],
+                        )
+                    nc.scalar.copy(out=out_sb[:, t, :], in_=back[:])
+                nc.sync.dma_start(out=group_rows(out, g), in_=out_sb[:])

@@ -49,6 +49,10 @@ def tile_advancedliquidneuralnetwork_pb_t_kernel(
         ident_bf16 = consts.tile([P, P], BF16)
         make_identity(nc, ident_bf16[:])
 
+        one = consts.tile([P, 1], F32)
+        nc.vector.memset(one[:], 1.0)
+        nc.scalar.sqrt(out=one[:], in_=one[:])
+
         def quantise_k_last(src, pick_words, words_out, scales_out, turn_ps):
             grouped = stage.tile([P, GROUP, 2], F32, align_bytes=64)
             for pair in range(2):
@@ -124,13 +128,10 @@ def tile_advancedliquidneuralnetwork_pb_t_kernel(
                 liq_scales = codes.tile([P, GROUP], U8, align_bytes=64)
                 quantise_k_last(liq_sb, contiguous_words, liq_words, liq_scales, turn_ps)
 
-                liq_bo = work.tile([P, TILES, H], F32)
-                nc.vector.tensor_tensor(
-                    out=liq_bo[:],
-                    in0=liq_sb[:],
-                    in1=bo_all[:].unsqueeze(1).to_broadcast([P, TILES, H]),
-                    op=ALU.add,
-                )
+                u = kept.tile([P, TILES, H], F32, name="u%d" % g)
+                u_groups.append(u)
+                for t in range(TILES):
+                    nc.gpsimd.tensor_tensor(out=u[:, t, :], in0=liq_sb[:, t, :], in1=bo_all[:], op=ALU.add)
 
                 vT = work.tile([P, TILES, GROUP], BF16)
                 for j in range(TILES):
@@ -146,7 +147,10 @@ def tile_advancedliquidneuralnetwork_pb_t_kernel(
                         out=vT[:, j, :], in_=vT_acc[:], func=ACT.Identity, bias=bv[:, j : j + 1]
                     )
                 v_grouped = work.tile([P, GROUP, TILES], BF16, align_bytes=64)
-                nc.vector.tensor_copy(out=v_grouped[:], in_=vT[:].rearrange("p j c -> p c j"))
+                nc.vector.tensor_copy(
+                    out=v_grouped[:].rearrange("p (c i) j -> p c j i", i=4),
+                    in_=vT[:].rearrange("p j (c i) -> p c j i", i=4),
+                )
                 v_words = codes.tile([P, GROUP], U32, align_bytes=64)
                 v_scales = codes.tile([P, GROUP], U8, align_bytes=64)
                 nc.vector.quantize_mx(
@@ -155,8 +159,6 @@ def tile_advancedliquidneuralnetwork_pb_t_kernel(
                     in_=v_grouped[:].rearrange("p c j -> p (c j)"),
                 )
 
-                u = kept.tile([P, TILES, H], F32, name="u%d" % g)
-                u_groups.append(u)
                 sum_u = work.tile([P, TILES], F32)
                 for t in range(TILES):
                     att = att_ps.tile([P, H], F32)
@@ -171,7 +173,7 @@ def tile_advancedliquidneuralnetwork_pb_t_kernel(
                         out=u[:, t, :],
                         in0=att[:],
                         scalar=1.0,
-                        in1=liq_bo[:, t, :],
+                        in1=u[:, t, :],
                         op0=ALU.mult,
                         op1=ALU.add,
                         accum_out=sum_u[:, t : t + 1],
@@ -213,9 +215,13 @@ def tile_advancedliquidneuralnetwork_pb_t_kernel(
                 out=gate[:], in0=vec_cols[:, 2 * TILES : 3 * TILES], scalar1=TAU_EPS
             )
             nc.vector.reciprocal(out=gate[:], in_=gate[:])
-            keep = consts.tile([P, TILES], F32)
+            tau_all = consts.tile([P, H], BF16)
+            nc.sync.dma_start(out=tau_all[:], in_=tau.partition_broadcast(P))
+            keep_all = consts.tile([P, H], F32)
+            nc.vector.tensor_scalar_add(out=keep_all[:], in0=tau_all[:], scalar1=TAU_EPS)
+            nc.vector.reciprocal(out=keep_all[:], in_=keep_all[:])
             nc.vector.tensor_scalar(
-                out=keep[:], in0=gate[:], scalar1=-1.0, scalar2=1.0, op0=ALU.mult, op1=ALU.add
+                out=keep_all[:], in0=keep_all[:], scalar1=-1.0, scalar2=1.0, op0=ALU.mult, op1=ALU.add
             )
 
         rstd = kept.tile([P, GROUPS * TILES], F32)
@@ -227,11 +233,10 @@ def tile_advancedliquidneuralnetwork_pb_t_kernel(
 
         with ExitStack() as second:
             work = second.enter_context(tc.tile_pool(name="work_c", bufs=2))
-            turn_ps = second.enter_context(tc.psum_pool(name="turn_c", bufs=1))
+            turn_ps = second.enter_context(tc.psum_pool(name="turn_c", bufs=2))
             xin_ps = second.enter_context(tc.psum_pool(name="xin", bufs=2))
-            hT_ps = second.enter_context(tc.psum_pool(name="hT", bufs=2))
             sT_ps = second.enter_context(tc.psum_pool(name="sT", bufs=2))
-            back_ps = second.enter_context(tc.psum_pool(name="back", bufs=1))
+            back_ps = second.enter_context(tc.psum_pool(name="back", bufs=2))
 
             for g in range(GROUPS):
                 x_sb = rows.tile([P, TILES, H], BF16)
@@ -242,18 +247,11 @@ def tile_advancedliquidneuralnetwork_pb_t_kernel(
                 x_scales = codes.tile([P, GROUP], U8, align_bytes=64)
                 quantise_k_last(x_sb, contiguous_words, x_words, x_scales, turn_ps)
 
-                hT = []
-                for pair in range(2):
-                    hT_pair = hT_ps.tile([P, 2, GROUP], BF16)
-                    hT.append(hT_pair)
-                    for i in range(2):
-                        j = 2 * pair + i
-                        for t in range(TILES):
-                            nc.tensor.transpose(
-                                out=hT_pair[:, i, t * P : (t + 1) * P],
-                                in_=h_sb[:, t, j * P : (j + 1) * P],
-                                identity=ident_bf16[:],
-                            )
+                h_kept = work.tile([P, TILES, H], F32)
+                for t in range(TILES):
+                    nc.gpsimd.tensor_tensor(
+                        out=h_kept[:, t, :], in0=h_sb[:, t, :], in1=keep_all[:], op=ALU.mult
+                    )
 
                 u = u_groups[g]
                 s = work.tile([P, TILES, H], F32)
@@ -285,7 +283,6 @@ def tile_advancedliquidneuralnetwork_pb_t_kernel(
 
                 tanhT = work.tile([P, TILES, GROUP], F32)
                 gatedT = work.tile([P, TILES, GROUP], F32)
-                outT = work.tile([P, TILES, GROUP], F32)
                 for j in range(TILES):
                     sT = sT_ps.tile([P, GROUP], F32)
                     for t in range(TILES):
@@ -297,16 +294,8 @@ def tile_advancedliquidneuralnetwork_pb_t_kernel(
                     nc.scalar.activation(
                         out=tanhT[:, j, :], in_=sT[:], func=ACT.Tanh, bias=tanh_bias[:, j : j + 1]
                     )
-                    nc.vector.tensor_scalar_mul(
-                        out=gatedT[:, j, :], in0=tanhT[:, j, :], scalar1=gate[:, j : j + 1]
-                    )
-                    nc.vector.scalar_tensor_tensor(
-                        out=outT[:, j, :],
-                        in0=hT[j // 2][:, j % 2, :],
-                        scalar=keep[:, j : j + 1],
-                        in1=gatedT[:, j, :],
-                        op0=ALU.mult,
-                        op1=ALU.add,
+                    nc.scalar.activation(
+                        out=gatedT[:, j, :], in_=tanhT[:, j, :], func=ACT.Copy, scale=gate[:, j : j + 1]
                     )
 
                 out_sb = work.tile([P, TILES, H], F32)
@@ -315,8 +304,8 @@ def tile_advancedliquidneuralnetwork_pb_t_kernel(
                     for j in range(TILES):
                         nc.tensor.transpose(
                             out=back[:, j * P : (j + 1) * P],
-                            in_=outT[:, j, t * P : (t + 1) * P],
+                            in_=gatedT[:, j, t * P : (t + 1) * P],
                             identity=ident_f32[:],
                         )
-                    nc.scalar.copy(out=out_sb[:, t, :], in_=back[:])
+                    nc.vector.tensor_tensor(out=out_sb[:, t, :], in0=back[:], in1=h_kept[:, t, :], op=ALU.add)
                 nc.sync.dma_start(out=group_rows(out, g), in_=out_sb[:])

@@ -43,6 +43,7 @@ def tile_advancedliquidneuralnetwork_pb_t_kernel(
         rows = whole.enter_context(tc.tile_pool(name="rows", bufs=3))
         stage = whole.enter_context(tc.tile_pool(name="stage", bufs=2))
         codes = whole.enter_context(tc.tile_pool(name="codes", bufs=2))
+        g_ps = whole.enter_context(tc.psum_pool(name="g", bufs=1))
 
         ident_f32 = consts.tile([P, P], F32)
         make_identity(nc, ident_f32[:])
@@ -98,6 +99,8 @@ def tile_advancedliquidneuralnetwork_pb_t_kernel(
         win_words = consts.tile([P, H], U32, align_bytes=64)
         win_scales = consts.tile([P, H], U8, align_bytes=64)
 
+        g_all = g_ps.tile([P, H], F32)
+
         u_groups = []
         neg_means = []
         sum_sq = kept.tile([P, GROUPS * TILES], F32)
@@ -106,7 +109,7 @@ def tile_advancedliquidneuralnetwork_pb_t_kernel(
             work = first.enter_context(tc.tile_pool(name="work_a", bufs=2))
             turn_ps = first.enter_context(tc.psum_pool(name="turn_a", bufs=2))
             vT_ps = first.enter_context(tc.psum_pool(name="vT", bufs=3))
-            att_ps = first.enter_context(tc.psum_pool(name="att", bufs=3))
+            att_ps = first.enter_context(tc.psum_pool(name="att", bufs=2))
 
             quantise_weight(
                 W_v.rearrange("(p j) k -> p j k", j=TILES), contiguous_words, wv_words, wv_scales, turn_ps
@@ -194,18 +197,16 @@ def tile_advancedliquidneuralnetwork_pb_t_kernel(
             quantise_weight(
                 W_in.rearrange("(a p) k -> p a k", p=P), contiguous_words, win_words, win_scales, turn_ps
             )
-            g_all = consts.tile([P, H], BF16)
-            nc.sync.dma_start(out=g_all[:], in_=g_att.partition_broadcast(P))
             vec_rows = consts.tile([P, P], BF16)
             nc.vector.memset(vec_rows[:], 0.0)
-            for n, vec in enumerate((b_in, beta_att, tau)):
+            for n, vec in enumerate((b_in, beta_att, tau, g_att)):
                 nc.sync.dma_start(
                     out=vec_rows[n * TILES : (n + 1) * TILES, :], in_=vec.rearrange("(j p) -> j p", p=P)
                 )
             vec_ps = turn_ps.tile([P, P], BF16, tag="turned")
             nc.tensor.transpose(out=vec_ps[:], in_=vec_rows[:], identity=ident_bf16[:])
-            vec_cols = consts.tile([P, 3 * TILES], F32)
-            nc.vector.tensor_copy(out=vec_cols[:], in_=vec_ps[:, 0 : 3 * TILES])
+            vec_cols = consts.tile([P, 4 * TILES], F32)
+            nc.vector.tensor_copy(out=vec_cols[:], in_=vec_ps[:, 0 : 4 * TILES])
             tanh_bias = consts.tile([P, TILES], F32)
             nc.vector.tensor_add(
                 out=tanh_bias[:], in0=vec_cols[:, 0:TILES], in1=vec_cols[:, TILES : 2 * TILES]
@@ -215,6 +216,15 @@ def tile_advancedliquidneuralnetwork_pb_t_kernel(
                 out=gate[:], in0=vec_cols[:, 2 * TILES : 3 * TILES], scalar1=TAU_EPS
             )
             nc.vector.reciprocal(out=gate[:], in_=gate[:])
+            g_repeated = consts.tile([P, TILES, P], F32)
+            nc.vector.tensor_copy(
+                out=g_repeated[:],
+                in_=vec_cols[:, 3 * TILES : 4 * TILES].unsqueeze(2).to_broadcast([P, TILES, P]),
+            )
+            for j in range(TILES):
+                nc.tensor.transpose(
+                    out=g_all[:, j * P : (j + 1) * P], in_=g_repeated[:, j, :], identity=ident_f32[:]
+                )
             tau_all = consts.tile([P, H], BF16)
             nc.sync.dma_start(out=tau_all[:], in_=tau.partition_broadcast(P))
             keep_all = consts.tile([P, H], F32)
@@ -233,7 +243,7 @@ def tile_advancedliquidneuralnetwork_pb_t_kernel(
 
         with ExitStack() as second:
             work = second.enter_context(tc.tile_pool(name="work_c", bufs=2))
-            turn_ps = second.enter_context(tc.psum_pool(name="turn_c", bufs=2))
+            turn_ps = second.enter_context(tc.psum_pool(name="turn_c", bufs=1))
             xin_ps = second.enter_context(tc.psum_pool(name="xin", bufs=2))
             sT_ps = second.enter_context(tc.psum_pool(name="sT", bufs=2))
             back_ps = second.enter_context(tc.psum_pool(name="back", bufs=2))

@@ -28,6 +28,9 @@ def tile_advancedliquidneuralnetwork_pb_t_kernel(
 ):
     nc = tc.nc
 
+    def live(g):
+        return 0 <= g < GROUPS
+
     def group_rows(dram, g):
         return dram[g * GROUP : (g + 1) * GROUP, :].rearrange("(p t) f -> p t f", t=TILES)
 
@@ -38,12 +41,12 @@ def tile_advancedliquidneuralnetwork_pb_t_kernel(
         return words.rearrange("r (p u) -> r u p", u=2)[:, u, :]
 
     with ExitStack() as whole:
+        whole.enter_context(tc.manual_schedule())
         consts = whole.enter_context(tc.tile_pool(name="consts", bufs=1))
         kept = whole.enter_context(tc.tile_pool(name="kept", bufs=1))
-        rows = whole.enter_context(tc.tile_pool(name="rows", bufs=3))
-        stage = whole.enter_context(tc.tile_pool(name="stage", bufs=2))
-        codes = whole.enter_context(tc.tile_pool(name="codes", bufs=2))
-        g_ps = whole.enter_context(tc.psum_pool(name="g", bufs=1))
+        h_rows_pool = whole.enter_context(tc.tile_pool(name="h_rows", bufs=2))
+        h_kept_pool = whole.enter_context(tc.tile_pool(name="h_kept", bufs=3))
+        to_scalar = whole.enter_context(tc.psum_pool(name="to_scalar", bufs=4))
 
         ident_f32 = consts.tile([P, P], F32)
         make_identity(nc, ident_f32[:])
@@ -53,33 +56,6 @@ def tile_advancedliquidneuralnetwork_pb_t_kernel(
         one = consts.tile([P, 1], F32)
         nc.vector.memset(one[:], 1.0)
         nc.scalar.sqrt(out=one[:], in_=one[:])
-
-        def quantise_k_last(src, pick_words, words_out, scales_out, turn_ps):
-            grouped = stage.tile([P, GROUP, 2], F32, align_bytes=64)
-            for pair in range(2):
-                turned = turn_ps.tile([P, 2, 2, P], F32)
-                for i in range(2):
-                    words = src[:, 2 * pair + i, :].bitcast(F32)
-                    for u in range(2):
-                        nc.tensor.transpose(
-                            out=turned[:, i, u, :], in_=pick_words(words, u), identity=ident_f32[:]
-                        )
-                nc.scalar.copy(
-                    out=grouped[:, 2 * pair * P : 2 * (pair + 1) * P, :].rearrange(
-                        "p (i c) u -> p i c u", i=2
-                    ),
-                    in_=turned[:].rearrange("p i u c -> p i c u"),
-                )
-            nc.vector.quantize_mx(
-                out=words_out[:].bitcast(FP8X4),
-                scales=scales_out[:],
-                in_=grouped[:].rearrange("p c u -> p (c u)").bitcast(BF16),
-            )
-
-        def quantise_weight(w_rows, pick_words, words_out, scales_out, turn_ps):
-            w_sb = stage.tile([P, TILES, H], BF16)
-            nc.sync.dma_start(out=w_sb[:], in_=w_rows)
-            quantise_k_last(w_sb, pick_words, words_out, scales_out, turn_ps)
 
         def mx_pass(acc, stationary, stationary_scales, moving, moving_scales):
             nc.tensor.matmul_mx(
@@ -92,83 +68,156 @@ def tile_advancedliquidneuralnetwork_pb_t_kernel(
                 stop=True,
             )
 
+        def turn(src, pick_words):
+            banks = []
+            for pair in range(2):
+                bank = to_scalar.tile([P, 2, 2, P], F32, tag="bank")
+                banks.append(bank)
+                for i in range(2):
+                    words = src[:, 2 * pair + i, :].bitcast(F32)
+                    for u in range(2):
+                        nc.tensor.transpose(
+                            out=bank[:, i, u, :], in_=pick_words(words, u), identity=ident_f32[:]
+                        )
+            return banks
+
+        def lay_side_by_side(banks, grouped):
+            for pair in range(2):
+                nc.scalar.copy(
+                    out=grouped[:, 2 * pair * P : 2 * (pair + 1) * P, :].rearrange(
+                        "p (i c) u -> p i c u", i=2
+                    ),
+                    in_=banks[pair][:].rearrange("p i u c -> p i c u"),
+                )
+
+        def quantise(grouped, words_out, scales_out):
+            nc.vector.quantize_mx(
+                out=words_out[:].bitcast(FP8X4),
+                scales=scales_out[:],
+                in_=grouped[:].rearrange("p c u -> p (c u)").bitcast(BF16),
+            )
+
         wv_words = consts.tile([P, H], U32, align_bytes=64)
         wv_scales = consts.tile([P, H], U8, align_bytes=64)
         wo_words = consts.tile([P, H], U32, align_bytes=64)
         wo_scales = consts.tile([P, H], U8, align_bytes=64)
         win_words = consts.tile([P, H], U32, align_bytes=64)
         win_scales = consts.tile([P, H], U8, align_bytes=64)
+        weights = [
+            (W_v.rearrange("(p j) k -> p j k", j=TILES), contiguous_words, wv_words, wv_scales),
+            (W_o.rearrange("(a p) k -> p a k", p=P), alternate_words, wo_words, wo_scales),
+            (W_in.rearrange("(a p) k -> p a k", p=P), contiguous_words, win_words, win_scales),
+        ]
 
-        g_all = g_ps.tile([P, H], F32)
+        def has_weight(n):
+            return 0 <= n < len(weights)
 
-        u_groups = []
-        neg_means = []
+        u_of = {}
+        neg_mean_of = {}
+        x_words_of = {}
+        x_scales_of = {}
         sum_sq = kept.tile([P, GROUPS * TILES], F32)
+        bo_all = consts.tile([P, H], F32)
+        keep_all = consts.tile([P, H], F32)
+        tanh_bias = consts.tile([P, TILES], F32)
+        gate = consts.tile([P, TILES], F32)
+        bv = consts.tile([P, TILES], F32)
 
         with ExitStack() as first:
+            rows = first.enter_context(tc.tile_pool(name="rows", bufs=3))
+            stage = first.enter_context(tc.tile_pool(name="stage", bufs=4))
+            codes = first.enter_context(tc.tile_pool(name="codes", bufs=2))
             work = first.enter_context(tc.tile_pool(name="work_a", bufs=2))
-            turn_ps = first.enter_context(tc.psum_pool(name="turn_a", bufs=2))
-            vT_ps = first.enter_context(tc.psum_pool(name="vT", bufs=3))
-            att_ps = first.enter_context(tc.psum_pool(name="att", bufs=2))
+            to_vector = first.enter_context(tc.psum_pool(name="to_vector_a", bufs=3))
+            g_pool = first.enter_context(tc.psum_pool(name="g", bufs=1))
 
-            quantise_weight(
-                W_v.rearrange("(p j) k -> p j k", j=TILES), contiguous_words, wv_words, wv_scales, turn_ps
-            )
-            bv_bf16 = consts.tile([P, TILES], BF16)
-            nc.sync.dma_start(out=bv_bf16[:], in_=b_v.rearrange("(p j) -> p j", j=TILES))
-            bv = consts.tile([P, TILES], F32)
-            nc.vector.tensor_copy(out=bv[:], in_=bv_bf16[:])
-            bo_all = consts.tile([P, H], BF16)
-            nc.sync.dma_start(out=bo_all[:], in_=b_o.partition_broadcast(P))
-            quantise_weight(
-                W_o.rearrange("(a p) k -> p a k", p=P), alternate_words, wo_words, wo_scales, turn_ps
-            )
+            liq_rows, x_rows, w_rows = {}, {}, {}
+            liq_banks, x_banks, w_banks = {}, {}, {}
+            liq_grouped, x_grouped, w_grouped = {}, {}, {}
+            liq_words_of, liq_scales_of = {}, {}
+            vT_of, v_grouped_of, v_words_of, v_scales_of = {}, {}, {}, {}
 
-            for g in range(GROUPS):
+            def load_rows(g):
                 liq_sb = rows.tile([P, TILES, H], BF16)
                 nc.sync.dma_start(out=liq_sb[:], in_=group_rows(liq, g))
-                liq_words = codes.tile([P, GROUP], U32, align_bytes=64)
-                liq_scales = codes.tile([P, GROUP], U8, align_bytes=64)
-                quantise_k_last(liq_sb, contiguous_words, liq_words, liq_scales, turn_ps)
+                liq_rows[g] = liq_sb
+                x_sb = rows.tile([P, TILES, H], BF16)
+                nc.sync.dma_start(out=x_sb[:], in_=group_rows(x, g))
+                x_rows[g] = x_sb
 
+            def load_weight(n):
+                w_sb = rows.tile([P, TILES, H], BF16)
+                nc.sync.dma_start(out=w_sb[:], in_=weights[n][0])
+                w_rows[n] = w_sb
+
+            def copy_out(banks):
+                grouped = stage.tile([P, GROUP, 2], F32, align_bytes=64)
+                lay_side_by_side(banks, grouped)
+                return grouped
+
+            def start_u(g):
                 u = kept.tile([P, TILES, H], F32, name="u%d" % g)
-                u_groups.append(u)
+                u_of[g] = u
                 for t in range(TILES):
-                    nc.gpsimd.tensor_tensor(out=u[:, t, :], in0=liq_sb[:, t, :], in1=bo_all[:], op=ALU.add)
+                    nc.gpsimd.tensor_tensor(
+                        out=u[:, t, :], in0=liq_rows[g][:, t, :], in1=bo_all[:], op=ALU.add
+                    )
 
+            def v_passes(g):
                 vT = work.tile([P, TILES, GROUP], BF16)
+                vT_of[g] = vT
                 for j in range(TILES):
-                    vT_acc = vT_ps.tile([P, GROUP], F32)
+                    vT_acc = to_scalar.tile([P, GROUP], F32, tag="bank")
                     mx_pass(
                         vT_acc[:],
                         wv_words[:, j * P : (j + 1) * P],
                         wv_scales[:, j * P : (j + 1) * P],
-                        liq_words[:],
-                        liq_scales[:],
+                        liq_words_of[g][:],
+                        liq_scales_of[g][:],
                     )
                     nc.scalar.activation(
                         out=vT[:, j, :], in_=vT_acc[:], func=ACT.Identity, bias=bv[:, j : j + 1]
                     )
+
+            def regroup_v(g):
                 v_grouped = work.tile([P, GROUP, TILES], BF16, align_bytes=64)
+                v_grouped_of[g] = v_grouped
                 nc.vector.tensor_copy(
                     out=v_grouped[:].rearrange("p (c i) j -> p c j i", i=4),
-                    in_=vT[:].rearrange("p j (c i) -> p c j i", i=4),
+                    in_=vT_of[g][:].rearrange("p j (c i) -> p c j i", i=4),
                 )
+
+            def quantise_v(g):
                 v_words = codes.tile([P, GROUP], U32, align_bytes=64)
                 v_scales = codes.tile([P, GROUP], U8, align_bytes=64)
+                v_words_of[g], v_scales_of[g] = v_words, v_scales
                 nc.vector.quantize_mx(
                     out=v_words[:].bitcast(FP8X4),
                     scales=v_scales[:],
-                    in_=v_grouped[:].rearrange("p c j -> p (c j)"),
+                    in_=v_grouped_of[g][:].rearrange("p c j -> p (c j)"),
                 )
 
+            def quantise_liq(g):
+                liq_words = codes.tile([P, GROUP], U32, align_bytes=64)
+                liq_scales = codes.tile([P, GROUP], U8, align_bytes=64)
+                liq_words_of[g], liq_scales_of[g] = liq_words, liq_scales
+                quantise(liq_grouped[g], liq_words, liq_scales)
+
+            def quantise_x(g):
+                x_words = kept.tile([P, GROUP], U32, align_bytes=64, name="x_words%d" % g)
+                x_scales = kept.tile([P, GROUP], U8, align_bytes=64, name="x_scales%d" % g)
+                x_words_of[g], x_scales_of[g] = x_words, x_scales
+                quantise(x_grouped[g], x_words, x_scales)
+
+            def add_att(g):
+                u = u_of[g]
                 sum_u = work.tile([P, TILES], F32)
                 for t in range(TILES):
-                    att = att_ps.tile([P, H], F32)
+                    att = to_vector.tile([P, H], F32, tag="bank")
                     mx_pass(
                         att[:],
-                        v_words[:, t * P : (t + 1) * P],
-                        v_scales[:, t * P : (t + 1) * P],
+                        v_words_of[g][:, t * P : (t + 1) * P],
+                        v_scales_of[g][:, t * P : (t + 1) * P],
                         wo_words[:],
                         wo_scales[:],
                     )
@@ -182,57 +231,117 @@ def tile_advancedliquidneuralnetwork_pb_t_kernel(
                         accum_out=sum_u[:, t : t + 1],
                     )
                 neg_mean = kept.tile([P, TILES], F32, name="neg_mean%d" % g)
-                neg_means.append(neg_mean)
+                neg_mean_of[g] = neg_mean
                 nc.vector.tensor_scalar_mul(out=neg_mean[:], in0=sum_u[:], scalar1=-1.0 / H)
+
+            def squares(g):
                 for t in range(TILES):
-                    squares = work.tile([P, H], BF16)
+                    squared = work.tile([P, H], BF16)
                     nc.scalar.activation(
-                        out=squares[:],
-                        in_=u[:, t, :],
+                        out=squared[:],
+                        in_=u_of[g][:, t, :],
                         func=ACT.Square,
-                        bias=neg_mean[:, t : t + 1],
+                        bias=neg_mean_of[g][:, t : t + 1],
                         accum_out=sum_sq[:, g * TILES + t : g * TILES + t + 1],
                     )
 
-            quantise_weight(
-                W_in.rearrange("(a p) k -> p a k", p=P), contiguous_words, win_words, win_scales, turn_ps
-            )
+            def scale_by_g(g):
+                for t in range(TILES):
+                    nc.vector.scalar_tensor_tensor(
+                        out=u_of[g][:, t, :],
+                        in0=u_of[g][:, t, :],
+                        scalar=neg_mean_of[g][:, t : t + 1],
+                        in1=g_all[:],
+                        op0=ALU.add,
+                        op1=ALU.mult,
+                    )
+
             vec_rows = consts.tile([P, P], BF16)
             nc.vector.memset(vec_rows[:], 0.0)
-            for n, vec in enumerate((b_in, beta_att, tau, g_att)):
+            vectors = (b_in, beta_att, tau, g_att, b_o)
+            for n, vec in enumerate(vectors):
                 nc.sync.dma_start(
                     out=vec_rows[n * TILES : (n + 1) * TILES, :], in_=vec.rearrange("(j p) -> j p", p=P)
                 )
-            vec_ps = turn_ps.tile([P, P], BF16, tag="turned")
-            nc.tensor.transpose(out=vec_ps[:], in_=vec_rows[:], identity=ident_bf16[:])
-            vec_cols = consts.tile([P, 4 * TILES], F32)
-            nc.vector.tensor_copy(out=vec_cols[:], in_=vec_ps[:, 0 : 4 * TILES])
-            tanh_bias = consts.tile([P, TILES], F32)
-            nc.vector.tensor_add(
-                out=tanh_bias[:], in0=vec_cols[:, 0:TILES], in1=vec_cols[:, TILES : 2 * TILES]
-            )
-            gate = consts.tile([P, TILES], F32)
-            nc.vector.tensor_scalar_add(
-                out=gate[:], in0=vec_cols[:, 2 * TILES : 3 * TILES], scalar1=TAU_EPS
-            )
-            nc.vector.reciprocal(out=gate[:], in_=gate[:])
-            g_repeated = consts.tile([P, TILES, P], F32)
+            bv_bf16 = consts.tile([P, TILES], BF16)
+            nc.sync.dma_start(out=bv_bf16[:], in_=b_v.rearrange("(p j) -> p j", j=TILES))
+            load_weight(0)
+            load_rows(0)
+            load_weight(1)
+            load_rows(1)
+            load_weight(2)
+
+            vec_bank = to_vector.tile([P, P], BF16, tag="bank")
+            nc.tensor.transpose(out=vec_bank[:], in_=vec_rows[:], identity=ident_bf16[:])
+            vec_cols = consts.tile([P, len(vectors), TILES], F32)
             nc.vector.tensor_copy(
-                out=g_repeated[:],
-                in_=vec_cols[:, 3 * TILES : 4 * TILES].unsqueeze(2).to_broadcast([P, TILES, P]),
+                out=vec_cols[:].rearrange("p n j -> p (n j)"), in_=vec_bank[:, 0 : len(vectors) * TILES]
             )
-            for j in range(TILES):
-                nc.tensor.transpose(
-                    out=g_all[:, j * P : (j + 1) * P], in_=g_repeated[:, j, :], identity=ident_f32[:]
-                )
-            tau_all = consts.tile([P, H], BF16)
-            nc.sync.dma_start(out=tau_all[:], in_=tau.partition_broadcast(P))
-            keep_all = consts.tile([P, H], F32)
-            nc.vector.tensor_scalar_add(out=keep_all[:], in0=tau_all[:], scalar1=TAU_EPS)
-            nc.vector.reciprocal(out=keep_all[:], in_=keep_all[:])
+            nc.vector.tensor_copy(out=bv[:], in_=bv_bf16[:])
+            nc.vector.tensor_add(out=tanh_bias[:], in0=vec_cols[:, 0, :], in1=vec_cols[:, 1, :])
+            nc.vector.tensor_scalar_add(out=gate[:], in0=vec_cols[:, 2, :], scalar1=TAU_EPS)
+            nc.vector.reciprocal(out=gate[:], in_=gate[:])
+            keep = consts.tile([P, TILES], F32)
             nc.vector.tensor_scalar(
-                out=keep_all[:], in0=keep_all[:], scalar1=-1.0, scalar2=1.0, op0=ALU.mult, op1=ALU.add
+                out=keep[:], in0=gate[:], scalar1=-1.0, scalar2=1.0, op0=ALU.mult, op1=ALU.add
             )
+            g_all = g_pool.tile([P, H], F32)
+
+            def spread(cols, bank):
+                repeated = stage.tile([P, TILES, P], F32)
+                nc.vector.tensor_copy(out=repeated[:], in_=cols.unsqueeze(2).to_broadcast([P, TILES, P]))
+                for j in range(TILES):
+                    nc.tensor.transpose(
+                        out=bank[:, j * P : (j + 1) * P], in_=repeated[:, j, :], identity=ident_f32[:]
+                    )
+
+            def spread_vectors():
+                bo_bank = to_vector.tile([P, H], F32, tag="bank")
+                spread(vec_cols[:, 4, :], bo_bank)
+                keep_bank = to_vector.tile([P, H], F32, tag="bank")
+                spread(keep[:], keep_bank)
+                spread(vec_cols[:, 3, :], g_all)
+                nc.vector.tensor_copy(out=bo_all[:], in_=bo_bank[:])
+                nc.vector.tensor_copy(out=keep_all[:], in_=keep_bank[:])
+
+            liq_banks[0] = turn(liq_rows[0], contiguous_words)
+            w_banks[0] = turn(w_rows[0], weights[0][1])
+
+            for i in range(GROUPS + 4):
+                if live(i):
+                    liq_grouped[i] = copy_out(liq_banks[i])
+                if has_weight(i):
+                    w_grouped[i] = copy_out(w_banks[i])
+                if live(i - 1):
+                    start_u(i - 1)
+                    v_passes(i - 1)
+                if live(i):
+                    x_banks[i] = turn(x_rows[i], contiguous_words)
+                    x_grouped[i] = copy_out(x_banks[i])
+                if live(i + 1):
+                    liq_banks[i + 1] = turn(liq_rows[i + 1], contiguous_words)
+                if has_weight(i + 1):
+                    w_banks[i + 1] = turn(w_rows[i + 1], weights[i + 1][1])
+                if live(i - 2):
+                    regroup_v(i - 2)
+                if live(i - 4):
+                    scale_by_g(i - 4)
+                if live(i - 2):
+                    quantise_v(i - 2)
+                if live(i):
+                    quantise_liq(i)
+                if has_weight(i):
+                    quantise(w_grouped[i], weights[i][2], weights[i][3])
+                if live(i - 1):
+                    quantise_x(i - 1)
+                if live(i - 2):
+                    add_att(i - 2)
+                if live(i - 3):
+                    squares(i - 3)
+                if live(i + 2):
+                    load_rows(i + 2)
+                if i == 0:
+                    spread_vectors()
 
         rstd = kept.tile([P, GROUPS * TILES], F32)
         nc.vector.tensor_scalar(
@@ -243,79 +352,102 @@ def tile_advancedliquidneuralnetwork_pb_t_kernel(
 
         with ExitStack() as second:
             work = second.enter_context(tc.tile_pool(name="work_c", bufs=2))
-            turn_ps = second.enter_context(tc.psum_pool(name="turn_c", bufs=1))
-            xin_ps = second.enter_context(tc.psum_pool(name="xin", bufs=2))
-            sT_ps = second.enter_context(tc.psum_pool(name="sT", bufs=2))
-            back_ps = second.enter_context(tc.psum_pool(name="back", bufs=2))
+            out_pool = second.enter_context(tc.tile_pool(name="out", bufs=4))
+            to_vector = second.enter_context(tc.psum_pool(name="to_vector_c", bufs=4))
 
-            for g in range(GROUPS):
-                x_sb = rows.tile([P, TILES, H], BF16)
-                nc.sync.dma_start(out=x_sb[:], in_=group_rows(x, g))
-                h_sb = rows.tile([P, TILES, H], BF16)
+            h_rows, h_kept_of = {}, {}
+            xin_of, s_of, sT_of, gatedT_of = {}, {}, {}, {}
+
+            def load_h(g):
+                h_sb = h_rows_pool.tile([P, TILES, H], BF16)
                 nc.sync.dma_start(out=h_sb[:], in_=group_rows(h, g))
-                x_words = codes.tile([P, GROUP], U32, align_bytes=64)
-                x_scales = codes.tile([P, GROUP], U8, align_bytes=64)
-                quantise_k_last(x_sb, contiguous_words, x_words, x_scales, turn_ps)
+                h_rows[g] = h_sb
 
-                h_kept = work.tile([P, TILES, H], F32)
+            def keep_h(g):
+                h_kept = h_kept_pool.tile([P, TILES, H], F32)
+                h_kept_of[g] = h_kept
                 for t in range(TILES):
                     nc.gpsimd.tensor_tensor(
-                        out=h_kept[:, t, :], in0=h_sb[:, t, :], in1=keep_all[:], op=ALU.mult
+                        out=h_kept[:, t, :], in0=h_rows[g][:, t, :], in1=keep_all[:], op=ALU.mult
                     )
 
-                u = u_groups[g]
-                s = work.tile([P, TILES, H], F32)
+            def xin_passes(g):
+                xin_of[g] = []
                 for t in range(TILES):
-                    xin = xin_ps.tile([P, H], F32)
+                    xin = to_vector.tile([P, H], F32, tag="bank")
+                    xin_of[g].append(xin)
                     mx_pass(
                         xin[:],
-                        x_words[:, t * P : (t + 1) * P],
-                        x_scales[:, t * P : (t + 1) * P],
+                        x_words_of[g][:, t * P : (t + 1) * P],
+                        x_scales_of[g][:, t * P : (t + 1) * P],
                         win_words[:],
                         win_scales[:],
                     )
-                    nc.vector.scalar_tensor_tensor(
-                        out=u[:, t, :],
-                        in0=u[:, t, :],
-                        scalar=neg_means[g][:, t : t + 1],
-                        in1=g_all[:],
-                        op0=ALU.add,
-                        op1=ALU.mult,
-                    )
+
+            def norm(g):
+                s = work.tile([P, TILES, H], F32)
+                s_of[g] = s
+                for t in range(TILES):
                     nc.vector.scalar_tensor_tensor(
                         out=s[:, t, :],
-                        in0=u[:, t, :],
+                        in0=u_of[g][:, t, :],
                         scalar=rstd[:, g * TILES + t : g * TILES + t + 1],
-                        in1=xin[:],
+                        in1=xin_of[g][t][:],
                         op0=ALU.mult,
                         op1=ALU.add,
                     )
 
-                tanhT = work.tile([P, TILES, GROUP], F32)
-                gatedT = work.tile([P, TILES, GROUP], F32)
+            def turn_s(g):
+                sT_of[g] = []
                 for j in range(TILES):
-                    sT = sT_ps.tile([P, GROUP], F32)
+                    sT = to_scalar.tile([P, GROUP], F32, tag="bank")
+                    sT_of[g].append(sT)
                     for t in range(TILES):
                         nc.tensor.transpose(
                             out=sT[:, t * P : (t + 1) * P],
-                            in_=s[:, t, j * P : (j + 1) * P],
+                            in_=s_of[g][:, t, j * P : (j + 1) * P],
                             identity=ident_f32[:],
                         )
+
+            def tanh_and_gate(g):
+                gatedT = work.tile([P, TILES, GROUP], F32)
+                gatedT_of[g] = gatedT
+                for j in range(TILES):
                     nc.scalar.activation(
-                        out=tanhT[:, j, :], in_=sT[:], func=ACT.Tanh, bias=tanh_bias[:, j : j + 1]
+                        out=gatedT[:, j, :], in_=sT_of[g][j][:], func=ACT.Tanh, bias=tanh_bias[:, j : j + 1]
                     )
                     nc.scalar.activation(
-                        out=gatedT[:, j, :], in_=tanhT[:, j, :], func=ACT.Copy, scale=gate[:, j : j + 1]
+                        out=gatedT[:, j, :], in_=gatedT[:, j, :], func=ACT.Copy, scale=gate[:, j : j + 1]
                     )
 
-                out_sb = work.tile([P, TILES, H], F32)
+            def finish(g):
                 for t in range(TILES):
-                    back = back_ps.tile([P, H], F32)
+                    back = to_vector.tile([P, H], F32, tag="bank")
                     for j in range(TILES):
                         nc.tensor.transpose(
                             out=back[:, j * P : (j + 1) * P],
-                            in_=gatedT[:, j, t * P : (t + 1) * P],
+                            in_=gatedT_of[g][:, j, t * P : (t + 1) * P],
                             identity=ident_f32[:],
                         )
-                    nc.vector.tensor_tensor(out=out_sb[:, t, :], in0=back[:], in1=h_kept[:, t, :], op=ALU.add)
-                nc.sync.dma_start(out=group_rows(out, g), in_=out_sb[:])
+                    out_sb = out_pool.tile([P, H], F32)
+                    nc.vector.tensor_tensor(out=out_sb[:], in0=back[:], in1=h_kept_of[g][:, t, :], op=ALU.add)
+                    nc.sync.dma_start(out=group_rows(out, g)[:, t, :], in_=out_sb[:])
+
+            load_h(0)
+            load_h(1)
+            keep_h(0)
+            xin_passes(0)
+            for i in range(GROUPS + 2):
+                if live(i + 2):
+                    load_h(i + 2)
+                if live(i):
+                    norm(i)
+                if live(i - 2):
+                    finish(i - 2)
+                if live(i + 1):
+                    keep_h(i + 1)
+                    xin_passes(i + 1)
+                if live(i - 1):
+                    tanh_and_gate(i - 1)
+                if live(i):
+                    turn_s(i)

from contextlib import ExitStack

import concourse.mybir as mybir
from concourse.masks import make_identity

F32 = mybir.dt.float32
BF16 = mybir.dt.bfloat16
U32 = mybir.dt.uint32
U8 = mybir.dt.uint8
FP8X4 = mybir.dt.float8_e4m3fn_x4
ALU = mybir.AluOpType
ACT = mybir.ActivationFunctionType

P = 128
B = 4096
H = 512
TILES = 4
GROUP = TILES * P
GROUPS = B // GROUP
LN_EPS = 1e-5
TAU_EPS = 1e-6

FLOPS = 3 * 2 * B * H * H


def tile_advancedliquidneuralnetwork_pb_t_kernel(
    tc, liq, h, x, W_in, b_in, W_v, b_v, W_o, b_o, g_att, beta_att, tau, out
):
    nc = tc.nc

    def live(g):
        return 0 <= g < GROUPS

    def group_rows(dram, g):
        return dram[g * GROUP : (g + 1) * GROUP, :].rearrange("(p t) f -> p t f", t=TILES)

    def contiguous_words(words, u):
        return words[:, u * P : (u + 1) * P]

    def alternate_words(words, u):
        return words.rearrange("r (p u) -> r u p", u=2)[:, u, :]

    with ExitStack() as whole:
        whole.enter_context(tc.manual_schedule())
        consts = whole.enter_context(tc.tile_pool(name="consts", bufs=1))
        kept = whole.enter_context(tc.tile_pool(name="kept", bufs=1))
        h_rows_pool = whole.enter_context(tc.tile_pool(name="h_rows", bufs=2))
        h_kept_pool = whole.enter_context(tc.tile_pool(name="h_kept", bufs=3))
        to_scalar = whole.enter_context(tc.psum_pool(name="to_scalar", bufs=4))

        ident_f32 = consts.tile([P, P], F32)
        make_identity(nc, ident_f32[:])
        ident_bf16 = consts.tile([P, P], BF16)
        make_identity(nc, ident_bf16[:])

        one = consts.tile([P, 1], F32)
        nc.vector.memset(one[:], 1.0)
        nc.scalar.sqrt(out=one[:], in_=one[:])

        def mx_pass(acc, stationary, stationary_scales, moving, moving_scales):
            nc.tensor.matmul_mx(
                out=acc,
                lhsT=stationary.bitcast(FP8X4),
                lhsT_scale=stationary_scales,
                rhs=moving.bitcast(FP8X4),
                rhs_scale=moving_scales,
                start=True,
                stop=True,
            )

        def turn(src, pick_words):
            banks = []
            for pair in range(2):
                bank = to_scalar.tile([P, 2, 2, P], F32, tag="bank")
                banks.append(bank)
                for i in range(2):
                    words = src[:, 2 * pair + i, :].bitcast(F32)
                    for u in range(2):
                        nc.tensor.transpose(
                            out=bank[:, i, u, :], in_=pick_words(words, u), identity=ident_f32[:]
                        )
            return banks

        def lay_side_by_side(banks, grouped):
            for pair in range(2):
                nc.scalar.copy(
                    out=grouped[:, 2 * pair * P : 2 * (pair + 1) * P, :].rearrange(
                        "p (i c) u -> p i c u", i=2
                    ),
                    in_=banks[pair][:].rearrange("p i u c -> p i c u"),
                )

        def quantise(grouped, words_out, scales_out):
            nc.vector.quantize_mx(
                out=words_out[:].bitcast(FP8X4),
                scales=scales_out[:],
                in_=grouped[:].rearrange("p c u -> p (c u)").bitcast(BF16),
            )

        wv_words = consts.tile([P, H], U32, align_bytes=64)
        wv_scales = consts.tile([P, H], U8, align_bytes=64)
        wo_words = consts.tile([P, H], U32, align_bytes=64)
        wo_scales = consts.tile([P, H], U8, align_bytes=64)
        win_words = consts.tile([P, H], U32, align_bytes=64)
        win_scales = consts.tile([P, H], U8, align_bytes=64)
        weights = [
            (W_v.rearrange("(p j) k -> p j k", j=TILES), contiguous_words, wv_words, wv_scales),
            (W_o.rearrange("(a p) k -> p a k", p=P), alternate_words, wo_words, wo_scales),
            (W_in.rearrange("(a p) k -> p a k", p=P), contiguous_words, win_words, win_scales),
        ]

        def has_weight(n):
            return 0 <= n < len(weights)

        u_of = {}
        neg_mean_of = {}
        x_words_of = {}
        x_scales_of = {}
        sum_sq = kept.tile([P, GROUPS * TILES], F32)
        bo_all = consts.tile([P, H], F32)
        keep_all = consts.tile([P, H], F32)
        tanh_bias = consts.tile([P, TILES], F32)
        gate = consts.tile([P, TILES], F32)
        bv = consts.tile([P, TILES], F32)

        with ExitStack() as first:
            rows = first.enter_context(tc.tile_pool(name="rows", bufs=3))
            stage = first.enter_context(tc.tile_pool(name="stage", bufs=4))
            codes = first.enter_context(tc.tile_pool(name="codes", bufs=2))
            work = first.enter_context(tc.tile_pool(name="work_a", bufs=2))
            to_vector = first.enter_context(tc.psum_pool(name="to_vector_a", bufs=3))
            g_pool = first.enter_context(tc.psum_pool(name="g", bufs=1))

            liq_rows, x_rows, w_rows = {}, {}, {}
            liq_banks, x_banks, w_banks = {}, {}, {}
            liq_grouped, x_grouped, w_grouped = {}, {}, {}
            liq_words_of, liq_scales_of = {}, {}
            vT_of, v_grouped_of, v_words_of, v_scales_of = {}, {}, {}, {}

            def load_rows(g):
                liq_sb = rows.tile([P, TILES, H], BF16)
                nc.sync.dma_start(out=liq_sb[:], in_=group_rows(liq, g))
                liq_rows[g] = liq_sb
                x_sb = rows.tile([P, TILES, H], BF16)
                nc.sync.dma_start(out=x_sb[:], in_=group_rows(x, g))
                x_rows[g] = x_sb

            def load_weight(n):
                w_sb = rows.tile([P, TILES, H], BF16)
                nc.sync.dma_start(out=w_sb[:], in_=weights[n][0])
                w_rows[n] = w_sb

            def copy_out(banks):
                grouped = stage.tile([P, GROUP, 2], F32, align_bytes=64)
                lay_side_by_side(banks, grouped)
                return grouped

            def start_u(g):
                u = kept.tile([P, TILES, H], F32, name="u%d" % g)
                u_of[g] = u
                for t in range(TILES):
                    nc.gpsimd.tensor_tensor(
                        out=u[:, t, :], in0=liq_rows[g][:, t, :], in1=bo_all[:], op=ALU.add
                    )

            def v_passes(g):
                vT = work.tile([P, TILES, GROUP], BF16)
                vT_of[g] = vT
                for j in range(TILES):
                    vT_acc = to_scalar.tile([P, GROUP], F32, tag="bank")
                    mx_pass(
                        vT_acc[:],
                        wv_words[:, j * P : (j + 1) * P],
                        wv_scales[:, j * P : (j + 1) * P],
                        liq_words_of[g][:],
                        liq_scales_of[g][:],
                    )
                    nc.scalar.activation(
                        out=vT[:, j, :], in_=vT_acc[:], func=ACT.Identity, bias=bv[:, j : j + 1]
                    )

            def regroup_v(g):
                v_grouped = work.tile([P, GROUP, TILES], BF16, align_bytes=64)
                v_grouped_of[g] = v_grouped
                nc.vector.tensor_copy(
                    out=v_grouped[:].rearrange("p (c i) j -> p c j i", i=4),
                    in_=vT_of[g][:].rearrange("p j (c i) -> p c j i", i=4),
                )

            def quantise_v(g):
                v_words = codes.tile([P, GROUP], U32, align_bytes=64)
                v_scales = codes.tile([P, GROUP], U8, align_bytes=64)
                v_words_of[g], v_scales_of[g] = v_words, v_scales
                nc.vector.quantize_mx(
                    out=v_words[:].bitcast(FP8X4),
                    scales=v_scales[:],
                    in_=v_grouped_of[g][:].rearrange("p c j -> p (c j)"),
                )

            def quantise_liq(g):
                liq_words = codes.tile([P, GROUP], U32, align_bytes=64)
                liq_scales = codes.tile([P, GROUP], U8, align_bytes=64)
                liq_words_of[g], liq_scales_of[g] = liq_words, liq_scales
                quantise(liq_grouped[g], liq_words, liq_scales)

            def quantise_x(g):
                x_words = kept.tile([P, GROUP], U32, align_bytes=64, name="x_words%d" % g)
                x_scales = kept.tile([P, GROUP], U8, align_bytes=64, name="x_scales%d" % g)
                x_words_of[g], x_scales_of[g] = x_words, x_scales
                quantise(x_grouped[g], x_words, x_scales)

            def add_att(g):
                u = u_of[g]
                sum_u = work.tile([P, TILES], F32)
                for t in range(TILES):
                    att = to_vector.tile([P, H], F32, tag="bank")
                    mx_pass(
                        att[:],
                        v_words_of[g][:, t * P : (t + 1) * P],
                        v_scales_of[g][:, t * P : (t + 1) * P],
                        wo_words[:],
                        wo_scales[:],
                    )
                    nc.vector.scalar_tensor_tensor(
                        out=u[:, t, :],
                        in0=att[:],
                        scalar=1.0,
                        in1=u[:, t, :],
                        op0=ALU.mult,
                        op1=ALU.add,
                        accum_out=sum_u[:, t : t + 1],
                    )
                neg_mean = kept.tile([P, TILES], F32, name="neg_mean%d" % g)
                neg_mean_of[g] = neg_mean
                nc.vector.tensor_scalar_mul(out=neg_mean[:], in0=sum_u[:], scalar1=-1.0 / H)

            def squares(g):
                for t in range(TILES):
                    squared = work.tile([P, H], BF16)
                    nc.scalar.activation(
                        out=squared[:],
                        in_=u_of[g][:, t, :],
                        func=ACT.Square,
                        bias=neg_mean_of[g][:, t : t + 1],
                        accum_out=sum_sq[:, g * TILES + t : g * TILES + t + 1],
                    )

            def scale_by_g(g):
                for t in range(TILES):
                    nc.vector.scalar_tensor_tensor(
                        out=u_of[g][:, t, :],
                        in0=u_of[g][:, t, :],
                        scalar=neg_mean_of[g][:, t : t + 1],
                        in1=g_all[:],
                        op0=ALU.add,
                        op1=ALU.mult,
                    )

            vec_rows = consts.tile([P, P], BF16)
            nc.vector.memset(vec_rows[:], 0.0)
            vectors = (b_in, beta_att, tau, g_att, b_o)
            for n, vec in enumerate(vectors):
                nc.sync.dma_start(
                    out=vec_rows[n * TILES : (n + 1) * TILES, :], in_=vec.rearrange("(j p) -> j p", p=P)
                )
            bv_bf16 = consts.tile([P, TILES], BF16)
            nc.sync.dma_start(out=bv_bf16[:], in_=b_v.rearrange("(p j) -> p j", j=TILES))
            load_weight(0)
            load_rows(0)
            load_weight(1)
            load_rows(1)
            load_weight(2)

            vec_bank = to_vector.tile([P, P], BF16, tag="bank")
            nc.tensor.transpose(out=vec_bank[:], in_=vec_rows[:], identity=ident_bf16[:])
            vec_cols = consts.tile([P, len(vectors), TILES], F32)
            nc.vector.tensor_copy(
                out=vec_cols[:].rearrange("p n j -> p (n j)"), in_=vec_bank[:, 0 : len(vectors) * TILES]
            )
            nc.vector.tensor_copy(out=bv[:], in_=bv_bf16[:])
            nc.vector.tensor_add(out=tanh_bias[:], in0=vec_cols[:, 0, :], in1=vec_cols[:, 1, :])
            nc.vector.tensor_scalar_add(out=gate[:], in0=vec_cols[:, 2, :], scalar1=TAU_EPS)
            nc.vector.reciprocal(out=gate[:], in_=gate[:])
            keep = consts.tile([P, TILES], F32)
            nc.vector.tensor_scalar(
                out=keep[:], in0=gate[:], scalar1=-1.0, scalar2=1.0, op0=ALU.mult, op1=ALU.add
            )
            g_all = g_pool.tile([P, H], F32)

            def spread(cols, bank):
                repeated = stage.tile([P, TILES, P], F32)
                nc.vector.tensor_copy(out=repeated[:], in_=cols.unsqueeze(2).to_broadcast([P, TILES, P]))
                for j in range(TILES):
                    nc.tensor.transpose(
                        out=bank[:, j * P : (j + 1) * P], in_=repeated[:, j, :], identity=ident_f32[:]
                    )

            def spread_vectors():
                bo_bank = to_vector.tile([P, H], F32, tag="bank")
                spread(vec_cols[:, 4, :], bo_bank)
                keep_bank = to_vector.tile([P, H], F32, tag="bank")
                spread(keep[:], keep_bank)
                spread(vec_cols[:, 3, :], g_all)
                nc.vector.tensor_copy(out=bo_all[:], in_=bo_bank[:])
                nc.vector.tensor_copy(out=keep_all[:], in_=keep_bank[:])

            liq_banks[0] = turn(liq_rows[0], contiguous_words)
            w_banks[0] = turn(w_rows[0], weights[0][1])

            for i in range(GROUPS + 4):
                if live(i):
                    liq_grouped[i] = copy_out(liq_banks[i])
                if has_weight(i):
                    w_grouped[i] = copy_out(w_banks[i])
                if live(i - 1):
                    start_u(i - 1)
                    v_passes(i - 1)
                if live(i):
                    x_banks[i] = turn(x_rows[i], contiguous_words)
                    x_grouped[i] = copy_out(x_banks[i])
                if live(i + 1):
                    liq_banks[i + 1] = turn(liq_rows[i + 1], contiguous_words)
                if has_weight(i + 1):
                    w_banks[i + 1] = turn(w_rows[i + 1], weights[i + 1][1])
                if live(i - 2):
                    regroup_v(i - 2)
                if live(i - 4):
                    scale_by_g(i - 4)
                if live(i - 2):
                    quantise_v(i - 2)
                if live(i):
                    quantise_liq(i)
                if has_weight(i):
                    quantise(w_grouped[i], weights[i][2], weights[i][3])
                if live(i - 1):
                    quantise_x(i - 1)
                if live(i - 2):
                    add_att(i - 2)
                if live(i - 3):
                    squares(i - 3)
                if live(i + 2):
                    load_rows(i + 2)
                if i == 0:
                    spread_vectors()

        rstd = kept.tile([P, GROUPS * TILES], F32)
        nc.vector.tensor_scalar(
            out=rstd[:], in0=sum_sq[:], scalar1=1.0 / H, scalar2=LN_EPS, op0=ALU.mult, op1=ALU.add
        )
        nc.scalar.sqrt(out=rstd[:], in_=rstd[:])
        nc.vector.reciprocal(out=rstd[:], in_=rstd[:])

        with ExitStack() as second:
            work = second.enter_context(tc.tile_pool(name="work_c", bufs=2))
            out_pool = second.enter_context(tc.tile_pool(name="out", bufs=4))
            to_vector = second.enter_context(tc.psum_pool(name="to_vector_c", bufs=4))

            h_rows, h_kept_of = {}, {}
            xin_of, s_of, sT_of, gatedT_of = {}, {}, {}, {}

            def load_h(g):
                h_sb = h_rows_pool.tile([P, TILES, H], BF16)
                nc.sync.dma_start(out=h_sb[:], in_=group_rows(h, g))
                h_rows[g] = h_sb

            def keep_h(g):
                h_kept = h_kept_pool.tile([P, TILES, H], F32)
                h_kept_of[g] = h_kept
                for t in range(TILES):
                    nc.gpsimd.tensor_tensor(
                        out=h_kept[:, t, :], in0=h_rows[g][:, t, :], in1=keep_all[:], op=ALU.mult
                    )

            def xin_passes(g):
                xin_of[g] = []
                for t in range(TILES):
                    xin = to_vector.tile([P, H], F32, tag="bank")
                    xin_of[g].append(xin)
                    mx_pass(
                        xin[:],
                        x_words_of[g][:, t * P : (t + 1) * P],
                        x_scales_of[g][:, t * P : (t + 1) * P],
                        win_words[:],
                        win_scales[:],
                    )

            def norm(g):
                s = work.tile([P, TILES, H], F32)
                s_of[g] = s
                for t in range(TILES):
                    nc.vector.scalar_tensor_tensor(
                        out=s[:, t, :],
                        in0=u_of[g][:, t, :],
                        scalar=rstd[:, g * TILES + t : g * TILES + t + 1],
                        in1=xin_of[g][t][:],
                        op0=ALU.mult,
                        op1=ALU.add,
                    )

            def turn_s(g):
                sT_of[g] = []
                for j in range(TILES):
                    sT = to_scalar.tile([P, GROUP], F32, tag="bank")
                    sT_of[g].append(sT)
                    for t in range(TILES):
                        nc.tensor.transpose(
                            out=sT[:, t * P : (t + 1) * P],
                            in_=s_of[g][:, t, j * P : (j + 1) * P],
                            identity=ident_f32[:],
                        )

            def tanh_and_gate(g):
                gatedT = work.tile([P, TILES, GROUP], F32)
                gatedT_of[g] = gatedT
                for j in range(TILES):
                    nc.scalar.activation(
                        out=gatedT[:, j, :], in_=sT_of[g][j][:], func=ACT.Tanh, bias=tanh_bias[:, j : j + 1]
                    )
                    nc.scalar.activation(
                        out=gatedT[:, j, :], in_=gatedT[:, j, :], func=ACT.Copy, scale=gate[:, j : j + 1]
                    )

            def finish(g):
                for t in range(TILES):
                    back = to_vector.tile([P, H], F32, tag="bank")
                    for j in range(TILES):
                        nc.tensor.transpose(
                            out=back[:, j * P : (j + 1) * P],
                            in_=gatedT_of[g][:, j, t * P : (t + 1) * P],
                            identity=ident_f32[:],
                        )
                    out_sb = out_pool.tile([P, H], F32)
                    nc.vector.tensor_tensor(out=out_sb[:], in0=back[:], in1=h_kept_of[g][:, t, :], op=ALU.add)
                    nc.sync.dma_start(out=group_rows(out, g)[:, t, :], in_=out_sb[:])

            load_h(0)
            load_h(1)
            keep_h(0)
            xin_passes(0)
            for i in range(GROUPS + 2):
                if live(i + 2):
                    load_h(i + 2)
                if live(i):
                    norm(i)
                if live(i - 2):
                    finish(i - 2)
                if live(i + 1):
                    keep_h(i + 1)
                    xin_passes(i + 1)
                if live(i - 1):
                    tanh_and_gate(i - 1)
                if live(i):
                    turn_s(i)
